import numpy as np
import ml_dtypes


def mxq(x, axis, fmt="e4m3"):
    dtype, down = {"e4m3": (ml_dtypes.float8_e4m3fn, 7), "e5m2": (ml_dtypes.float8_e5m2, 14)}[fmt]
    v = np.moveaxis(np.asarray(x, np.float32).astype(ml_dtypes.bfloat16).astype(np.float64), axis, -1)
    blocks = v.reshape(v.shape[:-1] + (-1, 32))
    amax = np.abs(blocks).max(-1, keepdims=True)
    byte = np.maximum(np.where(amax > 0, np.frexp(amax)[1] - 1 + 127, 0) - down, 1)
    scale = np.exp2(byte - 127.0)
    codes = (blocks / scale).astype(np.float32).astype(dtype).astype(np.float64)
    return np.moveaxis((codes * scale).reshape(v.shape), -1, axis)


WIDE = False


def mx_kscale(k):
    if not WIDE:
        return np.ones(k)
    levels = np.array([10, -10, 5, -5, 0])
    a = np.random.permutation(np.resize(levels, k // 512 * 4)).reshape(k // 512, 4)
    idx = np.arange(k)
    return np.exp2(a[idx // 512, idx % 128 // 32])


BF16 = ml_dtypes.bfloat16


def bf(x):
    return np.asarray(x, np.float32).astype(BF16)


def f64(x):
    return np.asarray(x).astype(np.float64)


B, STACK, TUBE, CH, IMG, PATCH, EMBED = 20, 16, 4, 1, 128, 16, 1024
GH = IMG // PATCH
GW = IMG // PATCH
GD = STACK // TUBE
K = TUBE * CH * PATCH * PATCH


def _sincos_1d(dim, pos):
    omega = 1.0 / (10000.0 ** (np.arange(dim // 2, dtype=np.float64) / (dim / 2.0)))
    out = pos[:, None].astype(np.float64) * omega[None, :]
    return np.concatenate([np.sin(out), np.cos(out)], axis=1)


def get_3d_sincos_pos_embed(grid_h, grid_w, grid_depth, embed_dim):
    dim_t = embed_dim // 4
    dim_s = embed_dim - dim_t
    emb_t = _sincos_1d(dim_t, np.arange(grid_depth))
    emb_h = _sincos_1d(dim_s // 2, np.arange(grid_h))
    emb_w = _sincos_1d(dim_s - dim_s // 2, np.arange(grid_w))
    emb_hw = np.concatenate([np.repeat(emb_h, grid_w, axis=0), np.tile(emb_w, (grid_h, 1))], axis=1)
    ns = grid_h * grid_w
    return np.concatenate([np.repeat(emb_t, ns, axis=0), np.tile(emb_hw, (grid_depth, 1))], axis=1)


def setup_inputs():
    s = mx_kscale(K)
    sv = s.reshape(TUBE, CH, PATCH, PATCH)[:, :, None, :, None, :]
    video = np.random.standard_normal((B, GD, TUBE, CH, GH, PATCH, GW, PATCH)) * sv
    return {"video": bf(video.reshape(B, STACK, CH, IMG, IMG)),
            "W": bf(np.random.standard_normal((EMBED, K)) / np.sqrt(K) / s[None, :]),
            "b": bf(np.random.standard_normal(EMBED) * 0.3),
            "pos_embed": bf(get_3d_sincos_pos_embed(GH, GW, GD, EMBED)[None])}


def reference(video, W, b, pos_embed):
    video = f64(video)
    B_, T, C, H, W_ = video.shape
    p = PATCH
    gh, gw = H // p, W_ // p
    ns = gh * gw
    x = video.reshape(B_ * T, C, gh, p, gw, p)
    x = x.transpose(0, 2, 4, 1, 3, 5)
    x = x.reshape(B_, T, ns, C * p * p)
    x = x.reshape(B_, GD, TUBE, ns, C * p * p)
    x = x.transpose(0, 1, 3, 2, 4)
    tubelets = x.reshape(B_, GD * ns, TUBE * C * p * p)
    tokens = (mxq(tubelets, 2, "e4m3") @ mxq(f64(W), 1, "e4m3").T) + f64(b) + f64(pos_embed)
    return tokens

@@ -1,0 +1,193 @@
+from contextlib import ExitStack
+
+import concourse.mybir as mybir
+from concourse.masks import make_identity
+
+F32 = mybir.dt.float32
+BF16 = mybir.dt.bfloat16
+U32 = mybir.dt.uint32
+U8 = mybir.dt.uint8
+FP8X4 = mybir.dt.float8_e4m3fn_x4
+ADD = mybir.AluOpType.add
+
+P = 128
+NB = 20
+EMB = 1024
+FLOPS = 2 * NB * 256 * 1024 * EMB
+
+
+def tile_tubeletembedding_t_kernel(tc, video, W, b, pos_embed, out):
+    nc = tc.nc
+    with ExitStack() as ctx:
+        const = ctx.enter_context(tc.tile_pool(name="const", bufs=1))
+        vids = ctx.enter_context(tc.tile_pool(name="vids", bufs=1))
+        work = ctx.enter_context(tc.tile_pool(name="work", bufs=3))
+        resp = ctx.enter_context(tc.tile_pool(name="resp", bufs=6))
+        pst = ctx.enter_context(tc.psum_pool(name="pst", bufs=2))
+        psa = ctx.enter_context(tc.psum_pool(name="psa", bufs=6))
+
+        raw = []
+
+        def load_video(b0, n):
+            t = vids.tile([P, n, 2048], BF16, name="vid%d" % b0)
+            nc.sync.dma_start(
+                out=t[:],
+                in_=video[b0 : b0 + n].rearrange("b f c (i py) w -> (f c i) b (py w)", py=16),
+            )
+            for h in range(n):
+                raw.append(t[:, h, :])
+
+        w_raw = []
+
+        def load_w(c):
+            t = const.tile([P, 2, 1024], BF16, name="wraw%d" % c)
+            nc.sync.dma_start(
+                out=t[:], in_=W[c * 256 : (c + 1) * 256, :].rearrange("(eb p) k -> p eb k", p=P)
+            )
+            w_raw.append(t)
+
+        load_video(0, 1)
+        load_w(0)
+        load_w(1)
+        pos_raw = const.tile([P, 2, EMB], BF16, name="pos_raw")
+        nc.sync.dma_start(
+            out=pos_raw[:], in_=pos_embed[0].rearrange("(m J) e -> m J e", J=2)
+        )
+        bias_bc = const.tile([P, EMB], BF16, name="bias_bc")
+        nc.sync.dma_start(out=bias_bc[:], in_=b.partition_broadcast(P))
+        load_w(2)
+        load_w(3)
+        load_video(1, 1)
+        for b0 in range(2, NB, 2):
+            load_video(b0, 2)
+
+        ident = const.tile([P, P], F32, name="ident")
+        make_identity(nc, ident[:])
+        perm = const.tile([P, P], F32, name="perm")
+        for g in range(2):
+            nc.vector.tensor_copy(
+                out=perm[:, g * 64 : (g + 1) * 64].rearrange("p (d i u) -> p d i u", d=4, i=8, u=2),
+                in_=ident[:].rearrange("p (d g u i) -> p g d i u", d=4, g=2, u=2, i=8)[:, g],
+            )
+
+        w_grp = const.tile([P, 2, 4 * EMB], BF16, name="w_grp", align_bytes=64)
+        w_code = const.tile([P, 2, EMB], U32, name="w_code", align_bytes=64)
+        w_scale = const.tile([P, 2, EMB], U8, name="w_scale", align_bytes=64)
+        posb = const.tile([P, 2, EMB], F32, name="posb")
+
+        re_t = {}
+        grp_t = {}
+        code_t = {}
+
+        def stage_e(bi):
+            re = work.tile([P, 1024], F32, name="re")
+            nc.scalar.copy(
+                out=re[:].rearrange("p (j py pw) -> p j py pw", j=8, py=16, pw=8),
+                in_=raw[bi].bitcast(F32).rearrange("p (py j pw) -> p j py pw", py=16, j=8, pw=8),
+            )
+            re_t[bi] = re
+
+        def stage_t(bi):
+            re = re_t[bi]
+            grp = work.tile([P, 2048], BF16, name="grp", align_bytes=64)
+            grp_t[bi] = grp
+            for J in range(2):
+                tp = pst.tile([P, 512], F32, name="tp")
+                for jj in range(4):
+                    j = 2 * jj + J
+                    nc.tensor.transpose(
+                        tp[:, jj * P : (jj + 1) * P], re[:, j * P : (j + 1) * P], perm[:]
+                    )
+                nc.scalar.copy(
+                    out=grp[:].bitcast(F32)[:, J * 512 : (J + 1) * 512].rearrange(
+                        "p (gd jj u) -> p gd jj u", gd=64, jj=4, u=2
+                    ),
+                    in_=tp[:].rearrange("p (jj gd u) -> p gd jj u", jj=4, gd=64, u=2),
+                )
+
+        def stage_q(bi):
+            xc = work.tile([P, 512], U32, name="xc", align_bytes=64)
+            xs = work.tile([P, 512], U8, name="xs", align_bytes=64)
+            nc.vector.quantize_mx(out=xc[:].bitcast(FP8X4), scales=xs[:], in_=grp_t[bi][:])
+            code_t[bi] = (xc, xs)
+
+        def stage_w(c):
+            wf = w_raw[c][:].bitcast(F32)
+            for g in range(2):
+                tp = pst.tile([P, 512], F32, name="tp")
+                for u in range(2):
+                    for ebl in range(2):
+                        q = u * 2 + ebl
+                        nc.tensor.transpose(
+                            tp[:, q * P : (q + 1) * P],
+                            wf[:, ebl, (g * 2 + u) * P : (g * 2 + u + 1) * P],
+                            ident[:],
+                        )
+                dst = w_grp[:].bitcast(F32)[:, g, c * 512 : (c + 1) * 512].rearrange(
+                    "p (e u) -> p e u", u=2
+                )
+                src = tp[:].rearrange("p (u e) -> p e u", u=2)
+                if g == 0:
+                    nc.vector.tensor_copy(out=dst, in_=src)
+                else:
+                    nc.scalar.copy(out=dst, in_=src)
+
+        def stage_wq(eh):
+            for g in range(2):
+                nc.vector.quantize_mx(
+                    out=w_code[:, g, eh * 512 : (eh + 1) * 512].bitcast(FP8X4),
+                    scales=w_scale[:, g, eh * 512 : (eh + 1) * 512],
+                    in_=w_grp[:, g, eh * 2048 : (eh + 1) * 2048],
+                )
+
+        def stage_m(bi, order):
+            xc, xs = code_t[bi]
+            res = resp.tile([P, 2, EMB], F32, name="res")
+            for J, eh in order:
+                acc = psa.tile([P, 512], F32, name="acc")
+                cols = slice(eh * 512, (eh + 1) * 512)
+                for g in range(2):
+                    m = slice((J * 2 + g) * P, (J * 2 + g + 1) * P)
+                    nc.tensor.matmul_mx(
+                        out=acc[:],
+                        lhsT=xc[:, m].bitcast(FP8X4),
+                        lhsT_scale=xs[:, m],
+                        rhs=w_code[:, g, cols].bitcast(FP8X4),
+                        rhs_scale=w_scale[:, g, cols],
+                        start=(g == 0),
+                        stop=(g == 1),
+                    )
+                nc.vector.tensor_tensor(out=res[:, J, cols], in0=acc[:], in1=posb[:, J, cols], op=ADD)
+            nc.sync.dma_start(
+                out=out[bi].rearrange("(m J) e -> m J e", J=2), in_=res[:]
+            )
+
+        stage_e(0)
+        stage_t(0)
+        stage_w(0)
+        stage_w(1)
+        stage_wq(0)
+        stage_q(0)
+        stage_e(1)
+        stage_t(1)
+        stage_w(2)
+        stage_w(3)
+        stage_wq(1)
+        for J, eh in ((0, 0), (1, 0), (0, 1), (1, 1)):
+            cols = slice(eh * 512, (eh + 1) * 512)
+            nc.gpsimd.tensor_tensor(
+                out=posb[:, J, cols], in0=pos_raw[:, J, cols], in1=bias_bc[:, cols], op=ADD
+            )
+        stage_e(2)
+
+        for s in range(NB):
+            if s + 3 < NB:
+                stage_e(s + 3)
+            if s + 2 < NB:
+                stage_t(s + 2)
+            if s + 1 < NB:
+                stage_q(s + 1)
+            if s == 0:
+                stage_m(s, ((0, 0), (1, 0), (0, 1), (1, 1)))
+            else:
+                stage_m(s, ((0, 0), (0, 1), (1, 0), (1, 1)))

@@ -5,6 +5,7 @@ from concourse.masks import make_identity
 
 F32 = mybir.dt.float32
 BF16 = mybir.dt.bfloat16
+I32 = mybir.dt.int32
 U32 = mybir.dt.uint32
 U8 = mybir.dt.uint8
 FP8X4 = mybir.dt.float8_e4m3fn_x4
@@ -15,16 +16,32 @@ NB = 20
 EMB = 1024
 FLOPS = 2 * NB * 256 * 1024 * EMB
 
+GROUPS = [[0], [1], [2], [3]] + [[x, x + 1] for x in range(4, NB, 2)]
+
 
 def tile_tubeletembedding_t_kernel(tc, video, W, b, pos_embed, out):
     nc = tc.nc
     with ExitStack() as ctx:
+        ctx.enter_context(tc.manual_schedule())
         const = ctx.enter_context(tc.tile_pool(name="const", bufs=1))
         vids = ctx.enter_context(tc.tile_pool(name="vids", bufs=1))
-        work = ctx.enter_context(tc.tile_pool(name="work", bufs=3))
-        resp = ctx.enter_context(tc.tile_pool(name="resp", bufs=6))
-        pst = ctx.enter_context(tc.psum_pool(name="pst", bufs=2))
-        psa = ctx.enter_context(tc.psum_pool(name="psa", bufs=6))
+        work = ctx.enter_context(tc.tile_pool(name="work", bufs=4))
+        resp = ctx.enter_context(tc.tile_pool(name="resp", bufs=8))
+        pst = ctx.enter_context(tc.psum_pool(name="pst", bufs=4))
+        psa = ctx.enter_context(tc.psum_pool(name="psa", bufs=4))
+
+        brow = const.tile([P, EMB], BF16, name="brow")
+        nc.vector.memset(brow[:].bitcast(I32), 0)
+        ones = const.tile([P, P], BF16, name="ones")
+        nc.vector.memset(ones[:], 1.0)
+        ident = const.tile([P, P], F32, name="ident")
+        make_identity(nc, ident[:])
+        perm = const.tile([P, P], F32, name="perm")
+        for g in range(2):
+            nc.vector.tensor_copy(
+                out=perm[:, g * 64 : (g + 1) * 64].rearrange("p (d i u) -> p d i u", d=4, i=8, u=2),
+                in_=ident[:].rearrange("p (d g u i) -> p g d i u", d=4, g=2, u=2, i=8)[:, g],
+            )
 
         raw = []
 
@@ -40,7 +57,7 @@ def tile_tubeletembedding_t_kernel(tc, video, W, b, pos_embed, out):
         w_raw = []
 
         def load_w(c):
-            t = const.tile([P, 2, 1024], BF16, name="wraw%d" % c)
+            t = resp.tile([P, 2, 1024], BF16, name="wraw%d" % c, tag="res", align_bytes=64)
             nc.sync.dma_start(
                 out=t[:], in_=W[c * 256 : (c + 1) * 256, :].rearrange("(eb p) k -> p eb k", p=P)
             )
@@ -48,46 +65,42 @@ def tile_tubeletembedding_t_kernel(tc, video, W, b, pos_embed, out):
 
         load_video(0, 1)
         load_w(0)
+        nc.sync.dma_start(out=brow[0:1, :], in_=b.rearrange("(o e) -> o e", o=1))
         load_w(1)
-        pos_raw = const.tile([P, 2, EMB], BF16, name="pos_raw")
-        nc.sync.dma_start(
-            out=pos_raw[:], in_=pos_embed[0].rearrange("(m J) e -> m J e", J=2)
-        )
-        bias_bc = const.tile([P, EMB], BF16, name="bias_bc")
-        nc.sync.dma_start(out=bias_bc[:], in_=b.partition_broadcast(P))
         load_w(2)
         load_w(3)
         load_video(1, 1)
-        for b0 in range(2, NB, 2):
+        pos_raw = const.tile([P, 2, EMB], BF16, name="pos_raw")
+        nc.sync.dma_start(out=pos_raw[:], in_=pos_embed[0].rearrange("(m J) e -> m J e", J=2))
+        load_video(2, 1)
+        load_video(3, 1)
+        for b0 in range(4, NB, 2):
             load_video(b0, 2)
 
-        ident = const.tile([P, P], F32, name="ident")
-        make_identity(nc, ident[:])
-        perm = const.tile([P, P], F32, name="perm")
-        for g in range(2):
-            nc.vector.tensor_copy(
-                out=perm[:, g * 64 : (g + 1) * 64].rearrange("p (d i u) -> p d i u", d=4, i=8, u=2),
-                in_=ident[:].rearrange("p (d g u i) -> p g d i u", d=4, g=2, u=2, i=8)[:, g],
-            )
-
-        w_grp = const.tile([P, 2, 4 * EMB], BF16, name="w_grp", align_bytes=64)
+        w_grp = [
+            resp.tile([P, 4 * EMB], BF16, name="w_grp%d" % g, tag="res", align_bytes=64)
+            for g in range(2)
+        ]
         w_code = const.tile([P, 2, EMB], U32, name="w_code", align_bytes=64)
         w_scale = const.tile([P, 2, EMB], U8, name="w_scale", align_bytes=64)
+        bias_bc = const.tile([P, EMB], F32, name="bias_bc")
         posb = const.tile([P, 2, EMB], F32, name="posb")
 
         re_t = {}
         grp_t = {}
         code_t = {}
 
-        def stage_e(bi):
+        def stage_e(bi, eng):
             re = work.tile([P, 1024], F32, name="re")
-            nc.scalar.copy(
-                out=re[:].rearrange("p (j py pw) -> p j py pw", j=8, py=16, pw=8),
-                in_=raw[bi].bitcast(F32).rearrange("p (py j pw) -> p j py pw", py=16, j=8, pw=8),
-            )
+            dst = re[:].rearrange("p (j py pw) -> p j py pw", j=8, py=16, pw=8)
+            src = raw[bi].bitcast(F32).rearrange("p (py j pw) -> p j py pw", py=16, j=8, pw=8)
+            if eng == "v":
+                nc.vector.tensor_copy(out=dst, in_=src)
+            else:
+                nc.scalar.copy(out=dst, in_=src)
             re_t[bi] = re
 
-        def stage_t(bi):
+        def stage_t(bi, engs):
             re = re_t[bi]
             grp = work.tile([P, 2048], BF16, name="grp", align_bytes=64)
             grp_t[bi] = grp
@@ -98,12 +111,14 @@ def tile_tubeletembedding_t_kernel(tc, video, W, b, pos_embed, out):
                     nc.tensor.transpose(
                         tp[:, jj * P : (jj + 1) * P], re[:, j * P : (j + 1) * P], perm[:]
                     )
-                nc.scalar.copy(
-                    out=grp[:].bitcast(F32)[:, J * 512 : (J + 1) * 512].rearrange(
-                        "p (gd jj u) -> p gd jj u", gd=64, jj=4, u=2
-                    ),
-                    in_=tp[:].rearrange("p (jj gd u) -> p gd jj u", jj=4, gd=64, u=2),
+                dst = grp[:].bitcast(F32)[:, J * 512 : (J + 1) * 512].rearrange(
+                    "p (gd jj u) -> p gd jj u", gd=64, jj=4, u=2
                 )
+                src = tp[:].rearrange("p (jj gd u) -> p gd jj u", jj=4, gd=64, u=2)
+                if engs[J] == "v":
+                    nc.vector.tensor_copy(out=dst, in_=src)
+                else:
+                    nc.scalar.copy(out=dst, in_=src)
 
         def stage_q(bi):
             xc = work.tile([P, 512], U32, name="xc", align_bytes=64)
@@ -123,7 +138,7 @@ def tile_tubeletembedding_t_kernel(tc, video, W, b, pos_embed, out):
                             wf[:, ebl, (g * 2 + u) * P : (g * 2 + u + 1) * P],
                             ident[:],
                         )
-                dst = w_grp[:].bitcast(F32)[:, g, c * 512 : (c + 1) * 512].rearrange(
+                dst = w_grp[g][:].bitcast(F32)[:, c * 512 : (c + 1) * 512].rearrange(
                     "p (e u) -> p e u", u=2
                 )
                 src = tp[:].rearrange("p (u e) -> p e u", u=2)
@@ -132,62 +147,73 @@ def tile_tubeletembedding_t_kernel(tc, video, W, b, pos_embed, out):
                 else:
                     nc.scalar.copy(out=dst, in_=src)
 
-        def stage_wq(eh):
+        def stage_wq(c):
             for g in range(2):
                 nc.vector.quantize_mx(
-                    out=w_code[:, g, eh * 512 : (eh + 1) * 512].bitcast(FP8X4),
-                    scales=w_scale[:, g, eh * 512 : (eh + 1) * 512],
-                    in_=w_grp[:, g, eh * 2048 : (eh + 1) * 2048],
+                    out=w_code[:, g, c * 256 : (c + 1) * 256].bitcast(FP8X4),
+                    scales=w_scale[:, g, c * 256 : (c + 1) * 256],
+                    in_=w_grp[g][:, c * 1024 : (c + 1) * 1024],
                 )
 
-        def stage_m(bi, order):
+        res_t = {}
+
+        def bank(bi, J, eh):
+            if (J, eh) == (0, 0):
+                res_t[bi] = resp.tile([P, 2, EMB], F32, name="res", tag="res", align_bytes=64)
+            res = res_t[bi]
             xc, xs = code_t[bi]
-            res = resp.tile([P, 2, EMB], F32, name="res")
-            for J, eh in order:
-                acc = psa.tile([P, 512], F32, name="acc")
-                cols = slice(eh * 512, (eh + 1) * 512)
-                for g in range(2):
-                    m = slice((J * 2 + g) * P, (J * 2 + g + 1) * P)
-                    nc.tensor.matmul_mx(
-                        out=acc[:],
-                        lhsT=xc[:, m].bitcast(FP8X4),
-                        lhsT_scale=xs[:, m],
-                        rhs=w_code[:, g, cols].bitcast(FP8X4),
-                        rhs_scale=w_scale[:, g, cols],
-                        start=(g == 0),
-                        stop=(g == 1),
-                    )
-                nc.vector.tensor_tensor(out=res[:, J, cols], in0=acc[:], in1=posb[:, J, cols], op=ADD)
-            nc.sync.dma_start(
-                out=out[bi].rearrange("(m J) e -> m J e", J=2), in_=res[:]
-            )
-
-        stage_e(0)
-        stage_t(0)
-        stage_w(0)
-        stage_w(1)
-        stage_wq(0)
-        stage_q(0)
-        stage_e(1)
-        stage_t(1)
-        stage_w(2)
-        stage_w(3)
-        stage_wq(1)
-        for J, eh in ((0, 0), (1, 0), (0, 1), (1, 1)):
+            acc = psa.tile([P, 512], F32, name="acc")
             cols = slice(eh * 512, (eh + 1) * 512)
-            nc.gpsimd.tensor_tensor(
-                out=posb[:, J, cols], in0=pos_raw[:, J, cols], in1=bias_bc[:, cols], op=ADD
-            )
-        stage_e(2)
+            for g in range(2):
+                m = slice((J * 2 + g) * P, (J * 2 + g + 1) * P)
+                nc.tensor.matmul_mx(
+                    out=acc[:],
+                    lhsT=xc[:, m].bitcast(FP8X4),
+                    lhsT_scale=xs[:, m],
+                    rhs=w_code[:, g, cols].bitcast(FP8X4),
+                    rhs_scale=w_scale[:, g, cols],
+                    start=(g == 0),
+                    stop=(g == 1),
+                )
+            nc.vector.tensor_tensor(out=res[:, J, cols], in0=acc[:], in1=posb[:, J, cols], op=ADD)
+            dram = out[bi].rearrange("(m J) e -> m J e", J=2)
+            if bi == NB - 1:
+                if eh == 1:
+                    nc.sync.dma_start(out=dram[:, J, :], in_=res[:, J, :])
+            elif (J, eh) == (1, 1):
+                nc.sync.dma_start(out=dram, in_=res[:])
 
-        for s in range(NB):
-            if s + 3 < NB:
-                stage_e(s + 3)
-            if s + 2 < NB:
-                stage_t(s + 2)
-            if s + 1 < NB:
-                stage_q(s + 1)
-            if s == 0:
-                stage_m(s, ((0, 0), (1, 0), (0, 1), (1, 1)))
-            else:
-                stage_m(s, ((0, 0), (0, 1), (1, 0), (1, 1)))
+        stage_e(0, "v")
+        stage_t(0, "vs")
+        stage_q(0)
+        for eh in range(2):
+            cols = slice(eh * 512, (eh + 1) * 512)
+            acc = psa.tile([P, 512], F32, name="acc")
+            nc.tensor.matmul(out=acc[:], lhsT=ones[:], rhs=brow[:, cols], start=True, stop=True)
+            nc.vector.tensor_copy(out=bias_bc[:, cols], in_=acc[:])
+        for c in range(4):
+            stage_w(c)
+            if c > 0:
+                stage_wq(c - 1)
+        stage_wq(3)
+        stage_e(1, "v")
+        for J in range(2):
+            for eh in range(2):
+                cols = slice(eh * 512, (eh + 1) * 512)
+                nc.gpsimd.tensor_tensor(
+                    out=posb[:, J, cols], in0=pos_raw[:, J, cols], in1=bias_bc[:, cols], op=ADD
+                )
+
+        for k in range(1, len(GROUPS) + 1):
+            g_now = GROUPS[k] if k < len(GROUPS) else []
+            g_next = GROUPS[k + 1] if k + 1 < len(GROUPS) else []
+            for bi in g_now:
+                stage_t(bi, "ss")
+            for bi in g_next:
+                stage_e(bi, "s")
+            banks = [(bi, J, eh) for bi in GROUPS[k - 1] for J in range(2) for eh in range(2)]
+            for n, bk in enumerate(banks):
+                if n == len(banks) // 2:
+                    for bi in g_now:
+                        stage_q(bi)
+                bank(bk[0], bk[1], bk[2])

@@ -16,6 +16,8 @@ NB = 20
 EMB = 1024
 FLOPS = 2 * NB * 256 * 1024 * EMB
 
+W_CHUNKS = [(0, 2), (256, 2), (512, 2), (768, 1), (896, 1)]
+FINE_STORES_FROM = 16
 GROUPS = [[0], [1], [2], [3]] + [[x, x + 1] for x in range(4, NB, 2)]
 
 
@@ -57,18 +59,18 @@ def tile_tubeletembedding_t_kernel(tc, video, W, b, pos_embed, out):
         w_raw = []
 
         def load_w(c):
-            t = resp.tile([P, 2, 1024], BF16, name="wraw%d" % c, tag="res", align_bytes=64)
+            row0, n_eb = W_CHUNKS[c]
+            t = resp.tile([P, n_eb, 1024], BF16, name="wraw%d" % c, tag="res", align_bytes=64)
             nc.sync.dma_start(
-                out=t[:], in_=W[c * 256 : (c + 1) * 256, :].rearrange("(eb p) k -> p eb k", p=P)
+                out=t[:],
+                in_=W[row0 : row0 + n_eb * P, :].rearrange("(eb p) k -> p eb k", p=P),
             )
             w_raw.append(t)
 
         load_video(0, 1)
-        load_w(0)
         nc.sync.dma_start(out=brow[0:1, :], in_=b.rearrange("(o e) -> o e", o=1))
-        load_w(1)
-        load_w(2)
-        load_w(3)
+        for c in range(len(W_CHUNKS)):
+            load_w(c)
         load_video(1, 1)
         pos_raw = const.tile([P, 2, EMB], BF16, name="pos_raw")
         nc.sync.dma_start(out=pos_raw[:], in_=pos_embed[0].rearrange("(m J) e -> m J e", J=2))
@@ -126,43 +128,46 @@ def tile_tubeletembedding_t_kernel(tc, video, W, b, pos_embed, out):
             nc.vector.quantize_mx(out=xc[:].bitcast(FP8X4), scales=xs[:], in_=grp_t[bi][:])
             code_t[bi] = (xc, xs)
 
-        def stage_w(c):
+        def stage_w(c, engs):
+            row0, n_eb = W_CHUNKS[c]
             wf = w_raw[c][:].bitcast(F32)
+            width = 2 * n_eb * P
             for g in range(2):
                 tp = pst.tile([P, 512], F32, name="tp")
                 for u in range(2):
-                    for ebl in range(2):
-                        q = u * 2 + ebl
+                    for ebl in range(n_eb):
+                        q = u * n_eb + ebl
                         nc.tensor.transpose(
                             tp[:, q * P : (q + 1) * P],
                             wf[:, ebl, (g * 2 + u) * P : (g * 2 + u + 1) * P],
                             ident[:],
                         )
-                dst = w_grp[g][:].bitcast(F32)[:, c * 512 : (c + 1) * 512].rearrange(
+                dst = w_grp[g][:].bitcast(F32)[:, row0 * 2 : row0 * 2 + width].rearrange(
                     "p (e u) -> p e u", u=2
                 )
-                src = tp[:].rearrange("p (u e) -> p e u", u=2)
-                if g == 0:
+                src = tp[:, 0:width].rearrange("p (u e) -> p e u", u=2)
+                if engs[g] == "v":
                     nc.vector.tensor_copy(out=dst, in_=src)
                 else:
                     nc.scalar.copy(out=dst, in_=src)
 
         def stage_wq(c):
+            row0, n_eb = W_CHUNKS[c]
+            n = n_eb * P
             for g in range(2):
                 nc.vector.quantize_mx(
-                    out=w_code[:, g, c * 256 : (c + 1) * 256].bitcast(FP8X4),
-                    scales=w_scale[:, g, c * 256 : (c + 1) * 256],
-                    in_=w_grp[g][:, c * 1024 : (c + 1) * 1024],
+                    out=w_code[:, g, row0 : row0 + n].bitcast(FP8X4),
+                    scales=w_scale[:, g, row0 : row0 + n],
+                    in_=w_grp[g][:, row0 * 4 : (row0 + n) * 4],
                 )
 
         res_t = {}
+        acc_t = {}
 
-        def bank(bi, J, eh):
-            if (J, eh) == (0, 0):
-                res_t[bi] = resp.tile([P, 2, EMB], F32, name="res", tag="res", align_bytes=64)
-            res = res_t[bi]
+        def mm(bi, J, eh):
             xc, xs = code_t[bi]
             acc = psa.tile([P, 512], F32, name="acc")
+            acc_t[(bi, J, eh)] = acc
             cols = slice(eh * 512, (eh + 1) * 512)
             for g in range(2):
                 m = slice((J * 2 + g) * P, (J * 2 + g + 1) * P)
@@ -175,36 +180,64 @@ def tile_tubeletembedding_t_kernel(tc, video, W, b, pos_embed, out):
                     start=(g == 0),
                     stop=(g == 1),
                 )
-            nc.vector.tensor_tensor(out=res[:, J, cols], in0=acc[:], in1=posb[:, J, cols], op=ADD)
+
+        def add_store(bi, J, eh):
+            if (J, eh) == (0, 0):
+                res_t[bi] = resp.tile([P, 2, EMB], F32, name="res", tag="res", align_bytes=64)
+            res = res_t[bi]
+            cols = slice(eh * 512, (eh + 1) * 512)
+            nc.vector.tensor_tensor(
+                out=res[:, J, cols], in0=acc_t[(bi, J, eh)][:], in1=posb[:, J, cols], op=ADD
+            )
             dram = out[bi].rearrange("(m J) e -> m J e", J=2)
-            if bi == NB - 1:
+            if bi >= FINE_STORES_FROM:
                 if eh == 1:
                     nc.sync.dma_start(out=dram[:, J, :], in_=res[:, J, :])
             elif (J, eh) == (1, 1):
                 nc.sync.dma_start(out=dram, in_=res[:])
 
-        stage_e(0, "v")
-        stage_t(0, "vs")
-        stage_q(0)
+        def posb_piece(eng, J, eh):
+            cols = slice(eh * 512, (eh + 1) * 512)
+            eng.tensor_tensor(
+                out=posb[:, J, cols], in0=pos_raw[:, J, cols], in1=bias_bc[:, cols], op=ADD
+            )
+
         for eh in range(2):
             cols = slice(eh * 512, (eh + 1) * 512)
             acc = psa.tile([P, 512], F32, name="acc")
             nc.tensor.matmul(out=acc[:], lhsT=ones[:], rhs=brow[:, cols], start=True, stop=True)
-            nc.vector.tensor_copy(out=bias_bc[:, cols], in_=acc[:])
-        for c in range(4):
-            stage_w(c)
-            if c > 0:
-                stage_wq(c - 1)
+            nc.scalar.copy(out=bias_bc[:, cols], in_=acc[:])
+        stage_e(0, "v")
+        stage_t(0, "vs")
+        stage_q(0)
+        stage_w(0, "vs")
+        stage_w(1, "ss")
+        stage_wq(0)
+        stage_w(2, "ss")
+        stage_wq(1)
+        stage_w(3, "vs")
+        stage_wq(2)
+        stage_w(4, "vs")
         stage_wq(3)
-        stage_e(1, "v")
-        for J in range(2):
-            for eh in range(2):
-                cols = slice(eh * 512, (eh + 1) * 512)
-                nc.gpsimd.tensor_tensor(
-                    out=posb[:, J, cols], in0=pos_raw[:, J, cols], in1=bias_bc[:, cols], op=ADD
-                )
+        stage_wq(4)
+        stage_e(1, "s")
+        posb_piece(nc.vector, 1, 1)
+        posb_piece(nc.gpsimd, 0, 0)
+        posb_piece(nc.gpsimd, 0, 1)
+        posb_piece(nc.gpsimd, 1, 0)
+        mm(0, 0, 0)
+        mm(0, 0, 1)
+        stage_t(1, "ss")
+        stage_e(2, "v")
+        mm(0, 1, 0)
+        mm(0, 1, 1)
+        add_store(0, 0, 0)
+        stage_q(1)
+        add_store(0, 0, 1)
+        add_store(0, 1, 0)
+        add_store(0, 1, 1)
 
-        for k in range(1, len(GROUPS) + 1):
+        for k in range(2, len(GROUPS) + 1):
             g_now = GROUPS[k] if k < len(GROUPS) else []
             g_next = GROUPS[k + 1] if k + 1 < len(GROUPS) else []
             for bi in g_now:
@@ -216,4 +249,5 @@ def tile_tubeletembedding_t_kernel(tc, video, W, b, pos_embed, out):
                 if n == len(banks) // 2:
                     for bi in g_now:
                         stage_q(bi)
-                bank(bk[0], bk[1], bk[2])
+                mm(bk[0], bk[1], bk[2])
+                add_store(bk[0], bk[1], bk[2])

@@ -181,14 +181,20 @@ def tile_tubeletembedding_t_kernel(tc, video, W, b, pos_embed, out):
                     stop=(g == 1),
                 )
 
-        def add_store(bi, J, eh):
+        def add_store(bi, J, eh, offload):
             if (J, eh) == (0, 0):
                 res_t[bi] = resp.tile([P, 2, EMB], F32, name="res", tag="res", align_bytes=64)
             res = res_t[bi]
             cols = slice(eh * 512, (eh + 1) * 512)
-            nc.vector.tensor_tensor(
-                out=res[:, J, cols], in0=acc_t[(bi, J, eh)][:], in1=posb[:, J, cols], op=ADD
-            )
+            if offload:
+                nc.scalar.copy(out=res[:, J, cols], in_=acc_t[(bi, J, eh)][:])
+                nc.gpsimd.tensor_tensor(
+                    out=res[:, J, cols], in0=res[:, J, cols], in1=posb[:, J, cols], op=ADD
+                )
+            else:
+                nc.vector.tensor_tensor(
+                    out=res[:, J, cols], in0=acc_t[(bi, J, eh)][:], in1=posb[:, J, cols], op=ADD
+                )
             dram = out[bi].rearrange("(m J) e -> m J e", J=2)
             if bi >= FINE_STORES_FROM:
                 if eh == 1:
@@ -223,19 +229,19 @@ def tile_tubeletembedding_t_kernel(tc, video, W, b, pos_embed, out):
         stage_e(1, "s")
         posb_piece(nc.vector, 1, 1)
         posb_piece(nc.gpsimd, 0, 0)
-        posb_piece(nc.gpsimd, 0, 1)
         posb_piece(nc.gpsimd, 1, 0)
+        posb_piece(nc.gpsimd, 0, 1)
         mm(0, 0, 0)
+        mm(0, 1, 0)
         mm(0, 0, 1)
         stage_t(1, "ss")
         stage_e(2, "v")
-        mm(0, 1, 0)
         mm(0, 1, 1)
-        add_store(0, 0, 0)
+        add_store(0, 0, 0, False)
         stage_q(1)
-        add_store(0, 0, 1)
-        add_store(0, 1, 0)
-        add_store(0, 1, 1)
+        add_store(0, 1, 0, False)
+        add_store(0, 0, 1, False)
+        add_store(0, 1, 1, False)
 
         for k in range(2, len(GROUPS) + 1):
             g_now = GROUPS[k] if k < len(GROUPS) else []
@@ -250,4 +256,4 @@ def tile_tubeletembedding_t_kernel(tc, video, W, b, pos_embed, out):
                     for bi in g_now:
                         stage_q(bi)
                 mm(bk[0], bk[1], bk[2])
-                add_store(bk[0], bk[1], bk[2])
+                add_store(bk[0], bk[1], bk[2], len(banks) == 8 and n == 6)

@@ -27,8 +27,8 @@ def tile_tubeletembedding_t_kernel(tc, video, W, b, pos_embed, out):
         ctx.enter_context(tc.manual_schedule())
         const = ctx.enter_context(tc.tile_pool(name="const", bufs=1))
         vids = ctx.enter_context(tc.tile_pool(name="vids", bufs=1))
-        work = ctx.enter_context(tc.tile_pool(name="work", bufs=4))
-        resp = ctx.enter_context(tc.tile_pool(name="resp", bufs=8))
+        work = ctx.enter_context(tc.tile_pool(name="work", bufs=3))
+        resp = ctx.enter_context(tc.tile_pool(name="resp", bufs=7))
         pst = ctx.enter_context(tc.psum_pool(name="pst", bufs=4))
         psa = ctx.enter_context(tc.psum_pool(name="psa", bufs=4))
 
@@ -38,23 +38,42 @@ def tile_tubeletembedding_t_kernel(tc, video, W, b, pos_embed, out):
         nc.vector.memset(ones[:], 1.0)
         ident = const.tile([P, P], F32, name="ident")
         make_identity(nc, ident[:])
-        perm = const.tile([P, P], F32, name="perm")
+        perm1 = const.tile([P, P], F32, name="perm1")
         for g in range(2):
             nc.vector.tensor_copy(
-                out=perm[:, g * 64 : (g + 1) * 64].rearrange("p (d i u) -> p d i u", d=4, i=8, u=2),
+                out=perm1[:, g * 64 : (g + 1) * 64].rearrange("p (d i u) -> p d i u", d=4, i=8, u=2),
                 in_=ident[:].rearrange("p (d g u i) -> p g d i u", d=4, g=2, u=2, i=8)[:, g],
             )
 
-        raw = []
+        perm2 = const.tile([P, P], F32, name="perm2")
+        for bb in range(2):
+            for g in range(2):
+                nc.vector.tensor_copy(
+                    out=perm2[:, bb * 64 + g * 32 : bb * 64 + (g + 1) * 32].rearrange(
+                        "p (d ih u) -> p d ih u", d=4, ih=4, u=2
+                    ),
+                    in_=ident[:].rearrange(
+                        "p (bb d g u ih) -> p bb g d ih u", bb=2, d=4, g=2, u=2, ih=4
+                    )[:, bb, g],
+                )
 
-        def load_video(b0, n):
-            t = vids.tile([P, n, 2048], BF16, name="vid%d" % b0)
+        raw = {}
+
+        def load_single(bi):
+            t = vids.tile([P, 2048], BF16, name="vid%d" % bi)
+            nc.sync.dma_start(
+                out=t[:], in_=video[bi].rearrange("f c (i py) w -> (f c i) (py w)", py=16)
+            )
+            raw[(bi, 0)] = t[:]
+
+        def load_pair(b0):
+            t = vids.tile([P, 4096], BF16, name="vid%d" % b0)
             nc.sync.dma_start(
                 out=t[:],
-                in_=video[b0 : b0 + n].rearrange("b f c (i py) w -> (f c i) b (py w)", py=16),
+                in_=video[b0 : b0 + 2].rearrange("b f c (ih r) w -> (b f c ih) (r w)", ih=4),
             )
-            for h in range(n):
-                raw.append(t[:, h, :])
+            for il in range(2):
+                raw[(b0, il)] = t[:, il * 2048 : (il + 1) * 2048]
 
         w_raw = []
 
@@ -63,21 +82,21 @@ def tile_tubeletembedding_t_kernel(tc, video, W, b, pos_embed, out):
             t = resp.tile([P, n_eb, 1024], BF16, name="wraw%d" % c, tag="res", align_bytes=64)
             nc.sync.dma_start(
                 out=t[:],
-                in_=W[row0 : row0 + n_eb * P, :].rearrange("(eb p) k -> p eb k", p=P),
+                in_=W[row0 : row0 + n_eb * P, :].rearrange("(p eb) k -> p eb k", eb=n_eb),
             )
             w_raw.append(t)
 
-        load_video(0, 1)
+        load_single(0)
         nc.sync.dma_start(out=brow[0:1, :], in_=b.rearrange("(o e) -> o e", o=1))
         for c in range(len(W_CHUNKS)):
             load_w(c)
-        load_video(1, 1)
+        load_single(1)
         pos_raw = const.tile([P, 2, EMB], BF16, name="pos_raw")
         nc.sync.dma_start(out=pos_raw[:], in_=pos_embed[0].rearrange("(m J) e -> m J e", J=2))
-        load_video(2, 1)
-        load_video(3, 1)
+        load_single(2)
+        load_single(3)
         for b0 in range(4, NB, 2):
-            load_video(b0, 2)
+            load_pair(b0)
 
         w_grp = [
             resp.tile([P, 4 * EMB], BF16, name="w_grp%d" % g, tag="res", align_bytes=64)
@@ -92,41 +111,59 @@ def tile_tubeletembedding_t_kernel(tc, video, W, b, pos_embed, out):
         grp_t = {}
         code_t = {}
 
-        def stage_e(bi, eng):
-            re = work.tile([P, 1024], F32, name="re")
-            dst = re[:].rearrange("p (j py pw) -> p j py pw", j=8, py=16, pw=8)
-            src = raw[bi].bitcast(F32).rearrange("p (py j pw) -> p j py pw", py=16, j=8, pw=8)
+        def copy(eng, dst, src):
             if eng == "v":
                 nc.vector.tensor_copy(out=dst, in_=src)
             else:
                 nc.scalar.copy(out=dst, in_=src)
-            re_t[bi] = re
 
-        def stage_t(bi, engs):
-            re = re_t[bi]
-            grp = work.tile([P, 2048], BF16, name="grp", align_bytes=64)
-            grp_t[bi] = grp
-            for J in range(2):
-                tp = pst.tile([P, 512], F32, name="tp")
-                for jj in range(4):
-                    j = 2 * jj + J
-                    nc.tensor.transpose(
-                        tp[:, jj * P : (jj + 1) * P], re[:, j * P : (j + 1) * P], perm[:]
+        def stage_e(key, eng):
+            re = work.tile([P, 1024], F32, name="re", bufs=4)
+            copy(
+                eng,
+                re[:].rearrange("p (j py pw) -> p j py pw", j=8, py=16, pw=8),
+                raw[key].bitcast(F32).rearrange("p (py j pw) -> p j py pw", py=16, j=8, pw=8),
+            )
+            re_t[key] = re
+
+        def stage_t(grp_list, engs):
+            b0 = grp_list[0]
+            n = len(grp_list)
+            grp = work.tile([P, n * 2048], BF16, name="grp", align_bytes=64)
+            grp_t[b0] = grp
+            dst_all = grp[:].bitcast(F32).rearrange(
+                "p (J x il yl u) -> p J il x yl u", J=2, x=64, il=n, yl=4, u=2
+            )
+            for il in range(n):
+                re = re_t[(b0, il)]
+                for J in range(2):
+                    tp = pst.tile([P, 512], F32, name="tp")
+                    for yl in range(4):
+                        j = 2 * yl + J
+                        nc.tensor.transpose(
+                            tp[:, yl * P : (yl + 1) * P],
+                            re[:, j * P : (j + 1) * P],
+                            perm1[:] if n == 1 else perm2[:],
+                        )
+                    copy(
+                        engs[J],
+                        dst_all[:, J, il],
+                        tp[:].rearrange("p (yl x u) -> p x yl u", yl=4, x=64, u=2),
                     )
-                dst = grp[:].bitcast(F32)[:, J * 512 : (J + 1) * 512].rearrange(
-                    "p (gd jj u) -> p gd jj u", gd=64, jj=4, u=2
-                )
-                src = tp[:].rearrange("p (jj gd u) -> p gd jj u", jj=4, gd=64, u=2)
-                if engs[J] == "v":
-                    nc.vector.tensor_copy(out=dst, in_=src)
-                else:
-                    nc.scalar.copy(out=dst, in_=src)
 
-        def stage_q(bi):
-            xc = work.tile([P, 512], U32, name="xc", align_bytes=64)
-            xs = work.tile([P, 512], U8, name="xs", align_bytes=64)
-            nc.vector.quantize_mx(out=xc[:].bitcast(FP8X4), scales=xs[:], in_=grp_t[bi][:])
-            code_t[bi] = (xc, xs)
+        def stage_q(grp_list):
+            b0 = grp_list[0]
+            n = len(grp_list)
+            xc = work.tile([P, n * 512], U32, name="xc", align_bytes=64)
+            xs = work.tile([P, n * 512], U8, name="xs", align_bytes=64)
+            for h in range(n):
+                nc.vector.quantize_mx(
+                    out=xc[:, h * 512 : (h + 1) * 512].bitcast(FP8X4),
+                    scales=xs[:, h * 512 : (h + 1) * 512],
+                    in_=grp_t[b0][:, h * 2048 : (h + 1) * 2048],
+                )
+            for bb in range(n):
+                code_t[b0 + bb] = (xc, xs, n, bb)
 
         def stage_w(c, engs):
             row0, n_eb = W_CHUNKS[c]
@@ -142,14 +179,13 @@ def tile_tubeletembedding_t_kernel(tc, video, W, b, pos_embed, out):
                             wf[:, ebl, (g * 2 + u) * P : (g * 2 + u + 1) * P],
                             ident[:],
                         )
-                dst = w_grp[g][:].bitcast(F32)[:, row0 * 2 : row0 * 2 + width].rearrange(
-                    "p (e u) -> p e u", u=2
+                copy(
+                    engs[g],
+                    w_grp[g][:].bitcast(F32)[:, row0 * 2 : row0 * 2 + width].rearrange(
+                        "p (e eb u) -> p e eb u", eb=n_eb, u=2
+                    ),
+                    tp[:, 0:width].rearrange("p (u eb e) -> p e eb u", u=2, eb=n_eb),
                 )
-                src = tp[:, 0:width].rearrange("p (u e) -> p e u", u=2)
-                if engs[g] == "v":
-                    nc.vector.tensor_copy(out=dst, in_=src)
-                else:
-                    nc.scalar.copy(out=dst, in_=src)
 
         def stage_wq(c):
             row0, n_eb = W_CHUNKS[c]
@@ -165,12 +201,13 @@ def tile_tubeletembedding_t_kernel(tc, video, W, b, pos_embed, out):
         acc_t = {}
 
         def mm(bi, J, eh):
-            xc, xs = code_t[bi]
+            xc, xs, n, bb = code_t[bi]
             acc = psa.tile([P, 512], F32, name="acc")
             acc_t[(bi, J, eh)] = acc
             cols = slice(eh * 512, (eh + 1) * 512)
             for g in range(2):
-                m = slice((J * 2 + g) * P, (J * 2 + g + 1) * P)
+                blk = (J * n + bb) * 2 + g
+                m = slice(blk * P, (blk + 1) * P)
                 nc.tensor.matmul_mx(
                     out=acc[:],
                     lhsT=xc[:, m].bitcast(FP8X4),
@@ -181,20 +218,14 @@ def tile_tubeletembedding_t_kernel(tc, video, W, b, pos_embed, out):
                     stop=(g == 1),
                 )
 
-        def add_store(bi, J, eh, offload):
+        def add_store(bi, J, eh):
             if (J, eh) == (0, 0):
                 res_t[bi] = resp.tile([P, 2, EMB], F32, name="res", tag="res", align_bytes=64)
             res = res_t[bi]
             cols = slice(eh * 512, (eh + 1) * 512)
-            if offload:
-                nc.scalar.copy(out=res[:, J, cols], in_=acc_t[(bi, J, eh)][:])
-                nc.gpsimd.tensor_tensor(
-                    out=res[:, J, cols], in0=res[:, J, cols], in1=posb[:, J, cols], op=ADD
-                )
-            else:
-                nc.vector.tensor_tensor(
-                    out=res[:, J, cols], in0=acc_t[(bi, J, eh)][:], in1=posb[:, J, cols], op=ADD
-                )
+            nc.vector.tensor_tensor(
+                out=res[:, J, cols], in0=acc_t[(bi, J, eh)][:], in1=posb[:, J, cols], op=ADD
+            )
             dram = out[bi].rearrange("(m J) e -> m J e", J=2)
             if bi >= FINE_STORES_FROM:
                 if eh == 1:
@@ -213,9 +244,9 @@ def tile_tubeletembedding_t_kernel(tc, video, W, b, pos_embed, out):
             acc = psa.tile([P, 512], F32, name="acc")
             nc.tensor.matmul(out=acc[:], lhsT=ones[:], rhs=brow[:, cols], start=True, stop=True)
             nc.scalar.copy(out=bias_bc[:, cols], in_=acc[:])
-        stage_e(0, "v")
-        stage_t(0, "vs")
-        stage_q(0)
+        stage_e((0, 0), "v")
+        stage_t([0], "vs")
+        stage_q([0])
         stage_w(0, "vs")
         stage_w(1, "ss")
         stage_wq(0)
@@ -226,34 +257,33 @@ def tile_tubeletembedding_t_kernel(tc, video, W, b, pos_embed, out):
         stage_w(4, "vs")
         stage_wq(3)
         stage_wq(4)
-        stage_e(1, "s")
-        posb_piece(nc.vector, 1, 1)
-        posb_piece(nc.gpsimd, 0, 0)
+        stage_e((1, 0), "s")
+        posb_piece(nc.vector, 0, 0)
+        posb_piece(nc.vector, 0, 1)
         posb_piece(nc.gpsimd, 1, 0)
-        posb_piece(nc.gpsimd, 0, 1)
+        posb_piece(nc.gpsimd, 1, 1)
         mm(0, 0, 0)
-        mm(0, 1, 0)
         mm(0, 0, 1)
-        stage_t(1, "ss")
-        stage_e(2, "v")
+        stage_t([1], "ss")
+        stage_e((2, 0), "v")
+        mm(0, 1, 0)
         mm(0, 1, 1)
-        add_store(0, 0, 0, False)
-        stage_q(1)
-        add_store(0, 1, 0, False)
-        add_store(0, 0, 1, False)
-        add_store(0, 1, 1, False)
+        add_store(0, 0, 0)
+        add_store(0, 0, 1)
+        stage_q([1])
+        add_store(0, 1, 0)
+        add_store(0, 1, 1)
 
         for k in range(2, len(GROUPS) + 1):
             g_now = GROUPS[k] if k < len(GROUPS) else []
             g_next = GROUPS[k + 1] if k + 1 < len(GROUPS) else []
-            for bi in g_now:
-                stage_t(bi, "ss")
-            for bi in g_next:
-                stage_e(bi, "s")
+            if g_now:
+                stage_t(g_now, "ss")
+            for il in range(len(g_next)):
+                stage_e((g_next[0], il), "s")
             banks = [(bi, J, eh) for bi in GROUPS[k - 1] for J in range(2) for eh in range(2)]
             for n, bk in enumerate(banks):
-                if n == len(banks) // 2:
-                    for bi in g_now:
-                        stage_q(bi)
+                if n == len(banks) // 2 and g_now:
+                    stage_q(g_now)
                 mm(bk[0], bk[1], bk[2])
-                add_store(bk[0], bk[1], bk[2], len(banks) == 8 and n == 6)
+                add_store(bk[0], bk[1], bk[2])

@@ -36,6 +36,8 @@ def tile_tubeletembedding_t_kernel(tc, video, W, b, pos_embed, out):
         nc.vector.memset(brow[:].bitcast(I32), 0)
         ones = const.tile([P, P], BF16, name="ones")
         nc.vector.memset(ones[:], 1.0)
+        warm_src = const.tile([P, 512], BF16, name="warm_src")
+        nc.vector.memset(warm_src[:], 1.0)
         ident = const.tile([P, P], F32, name="ident")
         make_identity(nc, ident[:])
         perm1 = const.tile([P, P], F32, name="perm1")
@@ -239,6 +241,12 @@ def tile_tubeletembedding_t_kernel(tc, video, W, b, pos_embed, out):
                 out=posb[:, J, cols], in0=pos_raw[:, J, cols], in1=bias_bc[:, cols], op=ADD
             )
 
+        def warm(tile_ap, count):
+            for rep in range(count):
+                nc.tensor.matmul(out=tile_ap, lhsT=ones[:], rhs=warm_src[:], start=True, stop=True)
+
+        warm_a = psa.tile([P, 512], F32, name="acc")
+        warm(warm_a[:], 8)
         for eh in range(2):
             cols = slice(eh * 512, (eh + 1) * 512)
             acc = psa.tile([P, 512], F32, name="acc")
@@ -247,14 +255,20 @@ def tile_tubeletembedding_t_kernel(tc, video, W, b, pos_embed, out):
         stage_e((0, 0), "v")
         stage_t([0], "vs")
         stage_q([0])
+        warm_b = psa.tile([P, 512], F32, name="acc")
         stage_w(0, "vs")
+        warm(warm_b[:], 1)
         stage_w(1, "ss")
+        warm(warm_b[:], 1)
         stage_wq(0)
         stage_w(2, "ss")
+        warm(warm_b[:], 1)
         stage_wq(1)
         stage_w(3, "vs")
+        warm(warm_b[:], 1)
         stage_wq(2)
         stage_w(4, "vs")
+        warm(warm_b[:], 3)
         stage_wq(3)
         stage_wq(4)
         stage_e((1, 0), "s")

from contextlib import ExitStack

import concourse.mybir as mybir
from concourse.masks import make_identity

F32 = mybir.dt.float32
BF16 = mybir.dt.bfloat16
I32 = mybir.dt.int32
U32 = mybir.dt.uint32
U8 = mybir.dt.uint8
FP8X4 = mybir.dt.float8_e4m3fn_x4
ADD = mybir.AluOpType.add

P = 128
NB = 20
EMB = 1024
FLOPS = 2 * NB * 256 * 1024 * EMB

W_CHUNKS = [(0, 2), (256, 2), (512, 2), (768, 1), (896, 1)]
FINE_STORES_FROM = 16
GROUPS = [[0], [1], [2], [3]] + [[x, x + 1] for x in range(4, NB, 2)]


def tile_tubeletembedding_t_kernel(tc, video, W, b, pos_embed, out):
    nc = tc.nc
    with ExitStack() as ctx:
        ctx.enter_context(tc.manual_schedule())
        const = ctx.enter_context(tc.tile_pool(name="const", bufs=1))
        vids = ctx.enter_context(tc.tile_pool(name="vids", bufs=1))
        work = ctx.enter_context(tc.tile_pool(name="work", bufs=3))
        resp = ctx.enter_context(tc.tile_pool(name="resp", bufs=7))
        pst = ctx.enter_context(tc.psum_pool(name="pst", bufs=4))
        psa = ctx.enter_context(tc.psum_pool(name="psa", bufs=4))

        brow = const.tile([P, EMB], BF16, name="brow")
        nc.vector.memset(brow[:].bitcast(I32), 0)
        ones = const.tile([P, P], BF16, name="ones")
        nc.vector.memset(ones[:], 1.0)
        warm_src = const.tile([P, 512], BF16, name="warm_src")
        nc.vector.memset(warm_src[:], 1.0)
        ident = const.tile([P, P], F32, name="ident")
        make_identity(nc, ident[:])
        perm1 = const.tile([P, P], F32, name="perm1")
        for g in range(2):
            nc.vector.tensor_copy(
                out=perm1[:, g * 64 : (g + 1) * 64].rearrange("p (d i u) -> p d i u", d=4, i=8, u=2),
                in_=ident[:].rearrange("p (d g u i) -> p g d i u", d=4, g=2, u=2, i=8)[:, g],
            )

        perm2 = const.tile([P, P], F32, name="perm2")
        for bb in range(2):
            for g in range(2):
                nc.vector.tensor_copy(
                    out=perm2[:, bb * 64 + g * 32 : bb * 64 + (g + 1) * 32].rearrange(
                        "p (d ih u) -> p d ih u", d=4, ih=4, u=2
                    ),
                    in_=ident[:].rearrange(
                        "p (bb d g u ih) -> p bb g d ih u", bb=2, d=4, g=2, u=2, ih=4
                    )[:, bb, g],
                )

        raw = {}

        def load_single(bi):
            t = vids.tile([P, 2048], BF16, name="vid%d" % bi)
            nc.sync.dma_start(
                out=t[:], in_=video[bi].rearrange("f c (i py) w -> (f c i) (py w)", py=16)
            )
            raw[(bi, 0)] = t[:]

        def load_pair(b0):
            t = vids.tile([P, 4096], BF16, name="vid%d" % b0)
            nc.sync.dma_start(
                out=t[:],
                in_=video[b0 : b0 + 2].rearrange("b f c (ih r) w -> (b f c ih) (r w)", ih=4),
            )
            for il in range(2):
                raw[(b0, il)] = t[:, il * 2048 : (il + 1) * 2048]

        w_raw = []

        def load_w(c):
            row0, n_eb = W_CHUNKS[c]
            t = resp.tile([P, n_eb, 1024], BF16, name="wraw%d" % c, tag="res", align_bytes=64)
            nc.sync.dma_start(
                out=t[:],
                in_=W[row0 : row0 + n_eb * P, :].rearrange("(p eb) k -> p eb k", eb=n_eb),
            )
            w_raw.append(t)

        load_single(0)
        nc.sync.dma_start(out=brow[0:1, :], in_=b.rearrange("(o e) -> o e", o=1))
        for c in range(len(W_CHUNKS)):
            load_w(c)
        load_single(1)
        pos_raw = const.tile([P, 2, EMB], BF16, name="pos_raw")
        nc.sync.dma_start(out=pos_raw[:], in_=pos_embed[0].rearrange("(m J) e -> m J e", J=2))
        load_single(2)
        load_single(3)
        for b0 in range(4, NB, 2):
            load_pair(b0)

        w_grp = [
            resp.tile([P, 4 * EMB], BF16, name="w_grp%d" % g, tag="res", align_bytes=64)
            for g in range(2)
        ]
        w_code = const.tile([P, 2, EMB], U32, name="w_code", align_bytes=64)
        w_scale = const.tile([P, 2, EMB], U8, name="w_scale", align_bytes=64)
        bias_bc = const.tile([P, EMB], F32, name="bias_bc")
        posb = const.tile([P, 2, EMB], F32, name="posb")

        re_t = {}
        grp_t = {}
        code_t = {}

        def copy(eng, dst, src):
            if eng == "v":
                nc.vector.tensor_copy(out=dst, in_=src)
            else:
                nc.scalar.copy(out=dst, in_=src)

        def stage_e(key, eng):
            re = work.tile([P, 1024], F32, name="re", bufs=4)
            copy(
                eng,
                re[:].rearrange("p (j py pw) -> p j py pw", j=8, py=16, pw=8),
                raw[key].bitcast(F32).rearrange("p (py j pw) -> p j py pw", py=16, j=8, pw=8),
            )
            re_t[key] = re

        def stage_t(grp_list, engs):
            b0 = grp_list[0]
            n = len(grp_list)
            grp = work.tile([P, n * 2048], BF16, name="grp", align_bytes=64)
            grp_t[b0] = grp
            dst_all = grp[:].bitcast(F32).rearrange(
                "p (J x il yl u) -> p J il x yl u", J=2, x=64, il=n, yl=4, u=2
            )
            for il in range(n):
                re = re_t[(b0, il)]
                for J in range(2):
                    tp = pst.tile([P, 512], F32, name="tp")
                    for yl in range(4):
                        j = 2 * yl + J
                        nc.tensor.transpose(
                            tp[:, yl * P : (yl + 1) * P],
                            re[:, j * P : (j + 1) * P],
                            perm1[:] if n == 1 else perm2[:],
                        )
                    copy(
                        engs[J],
                        dst_all[:, J, il],
                        tp[:].rearrange("p (yl x u) -> p x yl u", yl=4, x=64, u=2),
                    )

        def stage_q(grp_list):
            b0 = grp_list[0]
            n = len(grp_list)
            xc = work.tile([P, n * 512], U32, name="xc", align_bytes=64)
            xs = work.tile([P, n * 512], U8, name="xs", align_bytes=64)
            for h in range(n):
                nc.vector.quantize_mx(
                    out=xc[:, h * 512 : (h + 1) * 512].bitcast(FP8X4),
                    scales=xs[:, h * 512 : (h + 1) * 512],
                    in_=grp_t[b0][:, h * 2048 : (h + 1) * 2048],
                )
            for bb in range(n):
                code_t[b0 + bb] = (xc, xs, n, bb)

        def stage_w(c, engs):
            row0, n_eb = W_CHUNKS[c]
            wf = w_raw[c][:].bitcast(F32)
            width = 2 * n_eb * P
            for g in range(2):
                tp = pst.tile([P, 512], F32, name="tp")
                for u in range(2):
                    for ebl in range(n_eb):
                        q = u * n_eb + ebl
                        nc.tensor.transpose(
                            tp[:, q * P : (q + 1) * P],
                            wf[:, ebl, (g * 2 + u) * P : (g * 2 + u + 1) * P],
                            ident[:],
                        )
                copy(
                    engs[g],
                    w_grp[g][:].bitcast(F32)[:, row0 * 2 : row0 * 2 + width].rearrange(
                        "p (e eb u) -> p e eb u", eb=n_eb, u=2
                    ),
                    tp[:, 0:width].rearrange("p (u eb e) -> p e eb u", u=2, eb=n_eb),
                )

        def stage_wq(c):
            row0, n_eb = W_CHUNKS[c]
            n = n_eb * P
            for g in range(2):
                nc.vector.quantize_mx(
                    out=w_code[:, g, row0 : row0 + n].bitcast(FP8X4),
                    scales=w_scale[:, g, row0 : row0 + n],
                    in_=w_grp[g][:, row0 * 4 : (row0 + n) * 4],
                )

        res_t = {}
        acc_t = {}

        def mm(bi, J, eh):
            xc, xs, n, bb = code_t[bi]
            acc = psa.tile([P, 512], F32, name="acc")
            acc_t[(bi, J, eh)] = acc
            cols = slice(eh * 512, (eh + 1) * 512)
            for g in range(2):
                blk = (J * n + bb) * 2 + g
                m = slice(blk * P, (blk + 1) * P)
                nc.tensor.matmul_mx(
                    out=acc[:],
                    lhsT=xc[:, m].bitcast(FP8X4),
                    lhsT_scale=xs[:, m],
                    rhs=w_code[:, g, cols].bitcast(FP8X4),
                    rhs_scale=w_scale[:, g, cols],
                    start=(g == 0),
                    stop=(g == 1),
                )

        def add_store(bi, J, eh):
            if (J, eh) == (0, 0):
                res_t[bi] = resp.tile([P, 2, EMB], F32, name="res", tag="res", align_bytes=64)
            res = res_t[bi]
            cols = slice(eh * 512, (eh + 1) * 512)
            nc.vector.tensor_tensor(
                out=res[:, J, cols], in0=acc_t[(bi, J, eh)][:], in1=posb[:, J, cols], op=ADD
            )
            dram = out[bi].rearrange("(m J) e -> m J e", J=2)
            if bi >= FINE_STORES_FROM:
                if eh == 1:
                    nc.sync.dma_start(out=dram[:, J, :], in_=res[:, J, :])
            elif (J, eh) == (1, 1):
                nc.sync.dma_start(out=dram, in_=res[:])

        def posb_piece(eng, J, eh):
            cols = slice(eh * 512, (eh + 1) * 512)
            eng.tensor_tensor(
                out=posb[:, J, cols], in0=pos_raw[:, J, cols], in1=bias_bc[:, cols], op=ADD
            )

        def warm(tile_ap, count):
            for rep in range(count):
                nc.tensor.matmul(out=tile_ap, lhsT=ones[:], rhs=warm_src[:], start=True, stop=True)

        warm_a = psa.tile([P, 512], F32, name="acc")
        warm(warm_a[:], 8)
        for eh in range(2):
            cols = slice(eh * 512, (eh + 1) * 512)
            acc = psa.tile([P, 512], F32, name="acc")
            nc.tensor.matmul(out=acc[:], lhsT=ones[:], rhs=brow[:, cols], start=True, stop=True)
            nc.scalar.copy(out=bias_bc[:, cols], in_=acc[:])
        stage_e((0, 0), "v")
        stage_t([0], "vs")
        stage_q([0])
        warm_b = psa.tile([P, 512], F32, name="acc")
        stage_w(0, "vs")
        warm(warm_b[:], 1)
        stage_w(1, "ss")
        warm(warm_b[:], 1)
        stage_wq(0)
        stage_w(2, "ss")
        warm(warm_b[:], 1)
        stage_wq(1)
        stage_w(3, "vs")
        warm(warm_b[:], 1)
        stage_wq(2)
        stage_w(4, "vs")
        warm(warm_b[:], 3)
        stage_wq(3)
        stage_wq(4)
        stage_e((1, 0), "s")
        posb_piece(nc.vector, 0, 0)
        posb_piece(nc.vector, 0, 1)
        posb_piece(nc.gpsimd, 1, 0)
        posb_piece(nc.gpsimd, 1, 1)
        mm(0, 0, 0)
        mm(0, 0, 1)
        stage_t([1], "ss")
        stage_e((2, 0), "v")
        mm(0, 1, 0)
        mm(0, 1, 1)
        add_store(0, 0, 0)
        add_store(0, 0, 1)
        stage_q([1])
        add_store(0, 1, 0)
        add_store(0, 1, 1)

        for k in range(2, len(GROUPS) + 1):
            g_now = GROUPS[k] if k < len(GROUPS) else []
            g_next = GROUPS[k + 1] if k + 1 < len(GROUPS) else []
            if g_now:
                stage_t(g_now, "ss")
            for il in range(len(g_next)):
                stage_e((g_next[0], il), "s")
            banks = [(bi, J, eh) for bi in GROUPS[k - 1] for J in range(2) for eh in range(2)]
            for n, bk in enumerate(banks):
                if n == len(banks) // 2 and g_now:
                    stage_q(g_now)
                mm(bk[0], bk[1], bk[2])
                add_store(bk[0], bk[1], bk[2])
